import numpy as np
import ml_dtypes


def mxq(x, axis, fmt="e4m3"):
    dtype, down = {"e4m3": (ml_dtypes.float8_e4m3fn, 7), "e5m2": (ml_dtypes.float8_e5m2, 14)}[fmt]
    v = np.moveaxis(np.asarray(x, np.float32).astype(ml_dtypes.bfloat16).astype(np.float64), axis, -1)
    blocks = v.reshape(v.shape[:-1] + (-1, 32))
    amax = np.abs(blocks).max(-1, keepdims=True)
    byte = np.maximum(np.where(amax > 0, np.frexp(amax)[1] - 1 + 127, 0) - down, 1)
    scale = np.exp2(byte - 127.0)
    codes = (blocks / scale).astype(np.float32).astype(dtype).astype(np.float64)
    return np.moveaxis((codes * scale).reshape(v.shape), -1, axis)


WIDE = False


def mx_kscale(k):
    if not WIDE:
        return np.ones(k)
    levels = np.array([10, -10, 5, -5, 0])
    a = np.random.permutation(np.resize(levels, k // 512 * 4)).reshape(k // 512, 4)
    idx = np.arange(k)
    return np.exp2(a[idx // 512, idx % 128 // 32])


BF16 = ml_dtypes.bfloat16


def bf(x):
    return np.asarray(x, np.float32).astype(BF16)


def f64(x):
    return np.asarray(x).astype(np.float64)


E2M1 = np.array([0.0, 0.5, 1.0, 1.5, 2.0, 3.0, 4.0, 6.0, -0.0, -0.5, -1.0, -1.5, -2.0, -3.0, -4.0, -6.0])


def pack_weight(w, fmt):
    k, n = w.shape
    w = f64(bf(w)).reshape(k // 32, 32, n)
    amax = np.abs(w).max(1)
    if fmt == "e4m3":
        byte = np.frexp(amax)[1] - 1 + 127 - 7
    else:
        mant, ex = np.frexp(amax / 6.0)
        byte = np.where(mant > 0.5, ex, ex - 1) + 127
    byte = np.clip(np.where(amax > 0, byte, 1), 1, 254)
    scaled = (w * np.exp2(127.0 - byte)[:, None, :]).reshape(k, n).astype(np.float32)
    by_word = np.ascontiguousarray(scaled.reshape(k // 512, 128, 4, n).transpose(0, 1, 3, 2))
    if fmt == "e4m3":
        words = by_word.astype(ml_dtypes.float8_e4m3fn).view(np.uint8)
    else:
        c = by_word.astype(ml_dtypes.float4_e2m1fn).view(np.uint8) & 0xF
        words = c[..., 0::2] | (c[..., 1::2] << 4)
    return np.ascontiguousarray(words), np.ascontiguousarray(byte.astype(np.uint8).reshape(k // 512, 16, n))


def unpack_weight(words, scales, fmt):
    g, p, n, _ = words.shape
    if fmt == "e4m3":
        vals = np.ascontiguousarray(words).view(ml_dtypes.float8_e4m3fn).astype(np.float64)
    else:
        nib = np.empty((g, p, n, 4), np.uint8)
        nib[..., 0::2] = words & 0xF
        nib[..., 1::2] = words >> 4
        vals = E2M1[nib]
    vals = vals * np.repeat(np.exp2(scales.astype(np.float64) - 127.0), 8, axis=1)[..., None]
    return vals.transpose(0, 1, 3, 2).reshape(g * 512, n)

def pack4(w):
    words, scales = pack_weight(w, "e2m1")
    return words.reshape(words.shape[0], 128, -1), scales


def unpack4(words, scales):
    return unpack_weight(words.reshape(words.shape[0], 128, -1, 2), scales, "e2m1")


B, T, D, H, KVH, HD = 2, 2048, 512, 4, 2, 128
HALF = HD // 2
EPS = 1e-6
ROPE_BASE = 10000.0


def zc_rmsnorm(x, scale):
    rms = np.sqrt(np.mean(x ** 2, axis=-1, keepdims=True) + EPS)
    return (1.0 + scale) * x / rms


def apply_rope(x, cos, sin):
    t = x.shape[2]
    c = cos[:t][None, None, :, :]
    s = sin[:t][None, None, :, :]
    x1, x2 = x[..., :HALF], x[..., HALF:]
    return np.concatenate([x1 * c - x2 * s, x2 * c + x1 * s], axis=-1)


def setup_inputs():
    s = mx_kscale(D)
    inv_freq = 1.0 / (ROPE_BASE ** (np.arange(0, HALF) / HALF))
    ang = np.arange(T)[:, None] * inv_freq[None, :]
    kv_input = bf(np.random.standard_normal((B, T, D)) * s)
    Wk_words, Wk_scales = pack4(np.random.standard_normal((D, KVH * HD)) / np.sqrt(D) / s[:, None])
    Wv_words, Wv_scales = pack4(np.random.standard_normal((D, KVH * HD)) / np.sqrt(D) / s[:, None])
    return {"kv_input": kv_input,
            "Wk_words": Wk_words, "Wk_scales": Wk_scales,
            "Wv_words": Wv_words, "Wv_scales": Wv_scales,
            "k_scale": bf(np.random.standard_normal(HD) * 0.2),
            "cos": bf(np.cos(ang)), "sin": bf(np.sin(ang))}


def reference(kv_input, Wk_words, Wk_scales, Wv_words, Wv_scales, k_scale, cos, sin):
    b = kv_input.shape[0]
    xq = mxq(f64(kv_input), 2, "e4m3")
    k = (xq @ unpack4(Wk_words, Wk_scales)).reshape(b, -1, KVH, HD).transpose(0, 2, 1, 3)
    v = (xq @ unpack4(Wv_words, Wv_scales)).reshape(b, -1, KVH, HD).transpose(0, 2, 1, 3)
    k = zc_rmsnorm(k, f64(k_scale))
    rep = H // KVH
    k = np.repeat(k, rep, axis=1)
    v = np.repeat(v, rep, axis=1)
    k = apply_rope(k, f64(cos), f64(sin))
    return k, v

@@ -1,0 +1,242 @@
+from contextlib import ExitStack
+
+import concourse.mybir as mybir
+from concourse.masks import make_identity
+
+F32 = mybir.dt.float32
+BF16 = mybir.dt.bfloat16
+I32 = mybir.dt.int32
+U32 = mybir.dt.uint32
+U8 = mybir.dt.uint8
+FP8X4 = mybir.dt.float8_e4m3fn_x4
+FP4X4 = mybir.dt.float4_e2m1fn_x4
+ACT = mybir.ActivationFunctionType
+ALU = mybir.AluOpType
+
+P = 128
+BATCH, TOKENS, DIM = 2, 2048, 512
+KV_HEADS, HEAD_DIM = 2, 128
+COPIES = 2
+HALF = HEAD_DIM // 2
+KV_COLS = KV_HEADS * HEAD_DIM
+EPS = 1e-6
+
+WORDS = DIM // 2
+SLOTS = 8
+BLOCK_TOKENS = P * SLOTS
+PARTS = TOKENS // BLOCK_TOKENS
+GROUP = 4
+PAIR = 2
+
+FLOPS = 2 * BATCH * TOKENS * DIM * 2 * KV_COLS
+
+
+def tile_multiheadattention_pb_t_kernel(
+    tc, kv_input, Wk_words, Wk_scales, Wv_words, Wv_scales, k_scale, cos, sin, out_0, out_1
+):
+    nc = tc.nc
+    with ExitStack() as ctx:
+        const = ctx.enter_context(tc.tile_pool(name="const", bufs=1))
+        x_pool = ctx.enter_context(tc.tile_pool(name="x", bufs=BATCH * PARTS))
+        stage = ctx.enter_context(tc.tile_pool(name="stage", bufs=3))
+        small = ctx.enter_context(tc.tile_pool(name="small", bufs=4))
+        out_pool = ctx.enter_context(tc.tile_pool(name="outs", bufs=BATCH * PARTS))
+        xt_pool = ctx.enter_context(tc.psum_pool(name="xt", bufs=2))
+        k_pool = ctx.enter_context(tc.psum_pool(name="kacc", bufs=4))
+        v_pool = ctx.enter_context(tc.psum_pool(name="vacc", bufs=2))
+
+        blocks = [(b, part) for part in range(PARTS) for b in range(BATCH)]
+        groups = [(i, s0) for i in range(len(blocks)) for s0 in range(0, SLOTS, GROUP)]
+
+        identity = const.tile([P, P], F32)
+        make_identity(nc, identity[:])
+        ones = const.tile([P, P], BF16)
+        nc.vector.memset(ones[:], 1.0)
+        eps = const.tile([P, 1], F32)
+        nc.vector.memset(eps[:], EPS)
+        warm = const.tile([P, 1], F32)
+        nc.scalar.activation(out=warm[:], in_=eps[:], func=ACT.Sqrt)
+        w_planes = const.tile([P, 2 * KV_COLS], U8, align_bytes=64)
+        nc.vector.memset(w_planes[:].bitcast(I32), 0)
+        gain_row = const.tile([P, 2 * HEAD_DIM], BF16)
+        nc.vector.memset(gain_row[:], 0.0)
+
+        x_tiles = []
+        for i in range(len(blocks)):
+            x_sb = x_pool.tile([P, SLOTS, DIM], BF16, name="x_sb")
+            x_tiles.append(x_sb)
+
+        def load_x(i, s0):
+            b, part = blocks[i]
+            rows = kv_input[b, part * BLOCK_TOKENS : (part + 1) * BLOCK_TOKENS, :]
+            nc.sync.dma_start(
+                out=x_tiles[i][:, s0 : s0 + GROUP, :],
+                in_=rows.rearrange("(p s) k -> p s k", s=SLOTS)[:, s0 : s0 + GROUP, :],
+            )
+
+        load_x(*groups[0])
+        w_words = const.tile([P, 2, 2 * KV_COLS], U8, align_bytes=64)
+        for w, (words, scales) in enumerate(((Wk_words, Wk_scales), (Wv_words, Wv_scales))):
+            nc.sync.dma_start(out=w_words[:, w, :].bitcast(I32), in_=words[0].bitcast(I32))
+            for quadrant in range(4):
+                nc.sync.dma_start(
+                    out=w_planes[
+                        32 * quadrant : 32 * quadrant + 4, w * KV_COLS : (w + 1) * KV_COLS
+                    ].bitcast(I32),
+                    in_=scales[0, 4 * quadrant : 4 * quadrant + 4, :].bitcast(I32),
+                )
+        for rep in range(2):
+            nc.sync.dma_start(
+                out=gain_row[0:1, rep * HEAD_DIM : (rep + 1) * HEAD_DIM], in_=k_scale.unsqueeze(0)
+            )
+        cos_sin = const.tile([P, 2, PARTS, SLOTS, HALF], BF16)
+        for which, angle in enumerate((cos, sin)):
+            nc.sync.dma_start(
+                out=cos_sin[:, which],
+                in_=angle.rearrange("(h p s) j -> p h s j", h=PARTS, p=P),
+            )
+        for grp in groups[1:]:
+            load_x(*grp)
+
+        gain_ps = v_pool.tile([P, PAIR, KV_COLS], F32, tag="vacc")
+        nc.tensor.matmul(out=gain_ps[:, 0, :], lhsT=ones[:], rhs=gain_row[:], start=True, stop=True)
+        gains = const.tile([P, 2 * HEAD_DIM], F32)
+        plus = 2 * HEAD_DIM - HALF
+        nc.vector.tensor_scalar(
+            out=gains[:, 0:plus], in0=gain_ps[:, 0, 0:plus], scalar1=1.0, scalar2=None, op0=ALU.add
+        )
+        nc.vector.tensor_scalar(
+            out=gains[:, plus:],
+            in0=gain_ps[:, 0, plus:],
+            scalar1=-1.0,
+            scalar2=-1.0,
+            op0=ALU.mult,
+            op1=ALU.add,
+        )
+        table = const.tile([P, PARTS * SLOTS, 2, HEAD_DIM], F32)
+
+        def build_table(part, s0):
+            first = part * SLOTS + s0
+            for which in range(2):
+                nc.vector.tensor_tensor(
+                    out=table[:, first : first + GROUP, which, :].rearrange(
+                        "p s (h j) -> p s h j", h=2
+                    ),
+                    in0=cos_sin[:, which, part, s0 : s0 + GROUP, :]
+                    .unsqueeze(2)
+                    .to_broadcast([P, GROUP, 2, HALF]),
+                    in1=gains[:, which * HEAD_DIM : (which + 1) * HEAD_DIM]
+                    .rearrange("p (h j) -> p h j", h=2)
+                    .unsqueeze(1)
+                    .to_broadcast([P, GROUP, 2, HALF]),
+                    op=ALU.mult,
+                )
+
+        def quantise_group(i, s0):
+            grouped = stage.tile([P, GROUP * DIM], BF16, align_bytes=64)
+            grouped_words = grouped[:].bitcast(F32).rearrange("p (t r u) -> p t r u", t=GROUP, u=2)
+            for pair in range(0, GROUP, PAIR):
+                xt = xt_pool.tile([P, PAIR, 2, P], F32)
+                for t in range(PAIR):
+                    words = x_tiles[i][:, s0 + pair + t, :].bitcast(F32)
+                    for u in range(2):
+                        nc.tensor.transpose(xt[:, t, u, :], words[:, u:WORDS:2], identity[:])
+                nc.scalar.copy(
+                    out=grouped_words[:, pair : pair + PAIR],
+                    in_=xt[:].rearrange("p t u r -> p t r u"),
+                )
+            x_codes = stage.tile([P, GROUP * P], U32, align_bytes=64)
+            x_scales = stage.tile([P, GROUP * P], U8, align_bytes=64)
+            nc.vector.quantize_mx(out=x_codes[:].bitcast(FP8X4), scales=x_scales[:], in_=grouped[:])
+            return x_codes, x_scales
+
+        def project_group(i, s0, x_codes, x_scales, k_out, v_out):
+            part = blocks[i][1]
+            sumsq = small.tile([P, GROUP * KV_HEADS], F32)
+            k_banks = []
+            for pair in range(0, GROUP, PAIR):
+                k_acc = k_pool.tile([P, PAIR, KV_COLS], F32)
+                v_acc = v_pool.tile([P, PAIR, KV_COLS], F32, tag="vacc")
+                k_banks.append(k_acc)
+                for w, acc in enumerate((k_acc, v_acc)):
+                    for t in range(PAIR):
+                        tokens = slice((pair + t) * P, (pair + t + 1) * P)
+                        nc.tensor.matmul_mx(
+                            out=acc[:, t, :],
+                            lhsT=x_codes[:, tokens].bitcast(FP8X4),
+                            lhsT_scale=x_scales[:, tokens],
+                            rhs=w_words[:, w, :].bitcast(FP4X4),
+                            rhs_scale=w_planes[:, w * KV_COLS : (w + 1) * KV_COLS],
+                            start=True,
+                            stop=True,
+                        )
+                for t in range(PAIR):
+                    for g in range(KV_HEADS):
+                        squares = small.tile([P, HEAD_DIM], F32)
+                        col = (pair + t) * KV_HEADS + g
+                        nc.scalar.activation(
+                            out=squares[:],
+                            in_=k_acc[:, t, g * HEAD_DIM : (g + 1) * HEAD_DIM],
+                            func=ACT.Square,
+                            accum_out=sumsq[:, col : col + 1],
+                        )
+                nc.scalar.copy(
+                    out=v_out[:, :, s0 + pair : s0 + pair + PAIR, :].rearrange("p g t d -> p t g d"),
+                    in_=v_acc[:].rearrange("p t (g d) -> p t g d", g=KV_HEADS),
+                )
+            rms = small.tile([P, GROUP * KV_HEADS], F32)
+            nc.scalar.activation(
+                out=rms[:], in_=sumsq[:], func=ACT.Sqrt, scale=1.0 / HEAD_DIM, bias=eps[:, 0:1]
+            )
+            inv_rms = small.tile([P, GROUP * KV_HEADS], F32)
+            nc.vector.reciprocal(out=inv_rms[:], in_=rms[:])
+            products = stage.tile([P, KV_HEADS, GROUP, 2, HEAD_DIM], F32)
+            for t in range(GROUP):
+                for g in range(KV_HEADS):
+                    col = t * KV_HEADS + g
+                    nc.vector.scalar_tensor_tensor(
+                        out=products[:, g, t, :, :],
+                        in0=k_banks[t // PAIR][:, t % PAIR, g * HEAD_DIM : (g + 1) * HEAD_DIM]
+                        .unsqueeze(1)
+                        .to_broadcast([P, 2, HEAD_DIM]),
+                        scalar=inv_rms[:, col : col + 1],
+                        in1=table[:, part * SLOTS + s0 + t, :, :],
+                        op0=ALU.mult,
+                        op1=ALU.mult,
+                    )
+            for lo in (0, HALF):
+                other = HALF - lo
+                nc.gpsimd.tensor_tensor(
+                    out=k_out[:, :, s0 : s0 + GROUP, lo : lo + HALF],
+                    in0=products[:, :, :, 0, lo : lo + HALF],
+                    in1=products[:, :, :, 1, other : other + HALF],
+                    op=ALU.add,
+                )
+
+        def store(i, result, dram):
+            b, part = blocks[i]
+            heads = dram[b].rearrange("(g c) t d -> c g t d", c=COPIES)
+            for c in range(COPIES):
+                rows = heads[c][:, part * BLOCK_TOKENS : (part + 1) * BLOCK_TOKENS, :]
+                nc.sync.dma_start(
+                    out=rows.rearrange("g (p s) d -> p g (s d)", s=SLOTS),
+                    in_=result[:].rearrange("p g s d -> p g (s d)"),
+                )
+
+        outs = {}
+        ready = quantise_group(*groups[0])
+        for n, (i, s0) in enumerate(groups):
+            following = quantise_group(*groups[n + 1]) if n + 1 < len(groups) else None
+            b, part = blocks[i]
+            if b == 0:
+                build_table(part, s0)
+            if s0 == 0:
+                k_out = out_pool.tile([P, KV_HEADS, SLOTS, HEAD_DIM], F32, name="k_out")
+                v_out = out_pool.tile([P, KV_HEADS, SLOTS, HEAD_DIM], F32, name="v_out")
+                outs[i] = (k_out, v_out)
+            k_out, v_out = outs[i]
+            project_group(i, s0, ready[0], ready[1], k_out, v_out)
+            if s0 + GROUP == SLOTS:
+                store(i, v_out, out_1)
+                store(i, k_out, out_0)
+            ready = following

@@ -27,6 +27,7 @@ BLOCK_TOKENS = P * SLOTS
 PARTS = TOKENS // BLOCK_TOKENS
 GROUP = 4
 PAIR = 2
+BLOCKS_STORED_BY_GROUP = 1
 
 FLOPS = 2 * BATCH * TOKENS * DIM * 2 * KV_COLS
 
@@ -66,18 +67,15 @@ def tile_multiheadattention_pb_t_kernel(
             x_sb = x_pool.tile([P, SLOTS, DIM], BF16, name="x_sb")
             x_tiles.append(x_sb)
 
-        def load_x(i, s0):
+        def load_x(i, s0, slots):
             b, part = blocks[i]
             rows = kv_input[b, part * BLOCK_TOKENS : (part + 1) * BLOCK_TOKENS, :]
             nc.sync.dma_start(
-                out=x_tiles[i][:, s0 : s0 + GROUP, :],
-                in_=rows.rearrange("(p s) k -> p s k", s=SLOTS)[:, s0 : s0 + GROUP, :],
+                out=x_tiles[i][:, s0 : s0 + slots, :],
+                in_=rows.rearrange("(p s) k -> p s k", s=SLOTS)[:, s0 : s0 + slots, :],
             )
 
-        load_x(*groups[0])
-        w_words = const.tile([P, 2, 2 * KV_COLS], U8, align_bytes=64)
-        for w, (words, scales) in enumerate(((Wk_words, Wk_scales), (Wv_words, Wv_scales))):
-            nc.sync.dma_start(out=w_words[:, w, :].bitcast(I32), in_=words[0].bitcast(I32))
+        def load_scales(w, scales):
             for quadrant in range(4):
                 nc.sync.dma_start(
                     out=w_planes[
@@ -85,6 +83,14 @@ def tile_multiheadattention_pb_t_kernel(
                     ].bitcast(I32),
                     in_=scales[0, 4 * quadrant : 4 * quadrant + 4, :].bitcast(I32),
                 )
+
+        load_x(0, 0, GROUP)
+        w_words = const.tile([P, 2, 2 * KV_COLS], U8, align_bytes=64)
+        for w, words in enumerate((Wk_words, Wv_words)):
+            nc.sync.dma_start(out=w_words[:, w, :].bitcast(I32), in_=words[0].bitcast(I32))
+        load_scales(0, Wk_scales)
+        load_x(0, GROUP, SLOTS - GROUP)
+        load_scales(1, Wv_scales)
         for rep in range(2):
             nc.sync.dma_start(
                 out=gain_row[0:1, rep * HEAD_DIM : (rep + 1) * HEAD_DIM], in_=k_scale.unsqueeze(0)
@@ -95,8 +101,8 @@ def tile_multiheadattention_pb_t_kernel(
                 out=cos_sin[:, which],
                 in_=angle.rearrange("(h p s) j -> p h s j", h=PARTS, p=P),
             )
-        for grp in groups[1:]:
-            load_x(*grp)
+        for i in range(1, len(blocks)):
+            load_x(i, 0, SLOTS)
 
         gain_ps = v_pool.tile([P, PAIR, KV_COLS], F32, tag="vacc")
         nc.tensor.matmul(out=gain_ps[:, 0, :], lhsT=ones[:], rhs=gain_row[:], start=True, stop=True)
@@ -213,14 +219,14 @@ def tile_multiheadattention_pb_t_kernel(
                     op=ALU.add,
                 )
 
-        def store(i, result, dram):
+        def store(i, s0, slots, result, dram):
             b, part = blocks[i]
             heads = dram[b].rearrange("(g c) t d -> c g t d", c=COPIES)
             for c in range(COPIES):
                 rows = heads[c][:, part * BLOCK_TOKENS : (part + 1) * BLOCK_TOKENS, :]
                 nc.sync.dma_start(
-                    out=rows.rearrange("g (p s) d -> p g (s d)", s=SLOTS),
-                    in_=result[:].rearrange("p g s d -> p g (s d)"),
+                    out=rows.rearrange("g (p s) d -> p g s d", s=SLOTS)[:, :, s0 : s0 + slots, :],
+                    in_=result[:, :, s0 : s0 + slots, :],
                 )
 
         outs = {}
@@ -236,7 +242,10 @@ def tile_multiheadattention_pb_t_kernel(
                 outs[i] = (k_out, v_out)
             k_out, v_out = outs[i]
             project_group(i, s0, ready[0], ready[1], k_out, v_out)
-            if s0 + GROUP == SLOTS:
-                store(i, v_out, out_1)
-                store(i, k_out, out_0)
+            if i < BLOCKS_STORED_BY_GROUP:
+                store(i, s0, GROUP, v_out, out_1)
+                store(i, s0, GROUP, k_out, out_0)
+            elif s0 + GROUP == SLOTS:
+                store(i, 0, SLOTS, v_out, out_1)
+                store(i, 0, SLOTS, k_out, out_0)
             ready = following

@@ -25,11 +25,11 @@ WORDS = DIM // 2
 SLOTS = 8
 BLOCK_TOKENS = P * SLOTS
 PARTS = TOKENS // BLOCK_TOKENS
-GROUP = 4
 PAIR = 2
-BLOCKS_STORED_BY_GROUP = 1
+QUAD = 4
 
 FLOPS = 2 * BATCH * TOKENS * DIM * 2 * KV_COLS
+W_KEY, W_VALUE = 0, 1
 
 
 def tile_multiheadattention_pb_t_kernel(
@@ -38,16 +38,14 @@ def tile_multiheadattention_pb_t_kernel(
     nc = tc.nc
     with ExitStack() as ctx:
         const = ctx.enter_context(tc.tile_pool(name="const", bufs=1))
-        x_pool = ctx.enter_context(tc.tile_pool(name="x", bufs=BATCH * PARTS))
+        per_block = ctx.enter_context(tc.tile_pool(name="per_block", bufs=BATCH * PARTS))
         stage = ctx.enter_context(tc.tile_pool(name="stage", bufs=3))
         small = ctx.enter_context(tc.tile_pool(name="small", bufs=4))
-        out_pool = ctx.enter_context(tc.tile_pool(name="outs", bufs=BATCH * PARTS))
+        results = ctx.enter_context(tc.tile_pool(name="results", bufs=BATCH * PARTS * KV_HEADS))
         xt_pool = ctx.enter_context(tc.psum_pool(name="xt", bufs=2))
-        k_pool = ctx.enter_context(tc.psum_pool(name="kacc", bufs=4))
-        v_pool = ctx.enter_context(tc.psum_pool(name="vacc", bufs=2))
+        acc_pool = ctx.enter_context(tc.psum_pool(name="acc", bufs=6))
 
         blocks = [(b, part) for part in range(PARTS) for b in range(BATCH)]
-        groups = [(i, s0) for i in range(len(blocks)) for s0 in range(0, SLOTS, GROUP)]
 
         identity = const.tile([P, P], F32)
         make_identity(nc, identity[:])
@@ -62,10 +60,14 @@ def tile_multiheadattention_pb_t_kernel(
         gain_row = const.tile([P, 2 * HEAD_DIM], BF16)
         nc.vector.memset(gain_row[:], 0.0)
 
-        x_tiles = []
+        x_tiles, x_codes, x_scales = [], [], []
         for i in range(len(blocks)):
-            x_sb = x_pool.tile([P, SLOTS, DIM], BF16, name="x_sb")
+            x_sb = per_block.tile([P, SLOTS, DIM], BF16, name="x_sb")
+            codes = per_block.tile([P, SLOTS * P], U32, name="codes", align_bytes=64)
+            scales = per_block.tile([P, SLOTS * P], U8, name="scales", align_bytes=64)
             x_tiles.append(x_sb)
+            x_codes.append(codes)
+            x_scales.append(scales)
 
         def load_x(i, s0, slots):
             b, part = blocks[i]
@@ -84,64 +86,30 @@ def tile_multiheadattention_pb_t_kernel(
                     in_=scales[0, 4 * quadrant : 4 * quadrant + 4, :].bitcast(I32),
                 )
 
-        load_x(0, 0, GROUP)
         w_words = const.tile([P, 2, 2 * KV_COLS], U8, align_bytes=64)
-        for w, words in enumerate((Wk_words, Wv_words)):
+        cos_sin = const.tile([P, 2, PARTS, SLOTS, HALF], BF16)
+        load_x(0, 0, QUAD)
+        for w, words in ((W_VALUE, Wv_words), (W_KEY, Wk_words)):
             nc.sync.dma_start(out=w_words[:, w, :].bitcast(I32), in_=words[0].bitcast(I32))
-        load_scales(0, Wk_scales)
-        load_x(0, GROUP, SLOTS - GROUP)
-        load_scales(1, Wv_scales)
+        load_scales(W_VALUE, Wv_scales)
+        for s0 in range(QUAD, SLOTS, QUAD):
+            load_x(0, s0, QUAD)
         for rep in range(2):
             nc.sync.dma_start(
                 out=gain_row[0:1, rep * HEAD_DIM : (rep + 1) * HEAD_DIM], in_=k_scale.unsqueeze(0)
             )
-        cos_sin = const.tile([P, 2, PARTS, SLOTS, HALF], BF16)
         for which, angle in enumerate((cos, sin)):
             nc.sync.dma_start(
-                out=cos_sin[:, which],
-                in_=angle.rearrange("(h p s) j -> p h s j", h=PARTS, p=P),
+                out=cos_sin[:, which], in_=angle.rearrange("(h p s) j -> p h s j", h=PARTS, p=P)
             )
+        load_scales(W_KEY, Wk_scales)
         for i in range(1, len(blocks)):
             load_x(i, 0, SLOTS)
 
-        gain_ps = v_pool.tile([P, PAIR, KV_COLS], F32, tag="vacc")
-        nc.tensor.matmul(out=gain_ps[:, 0, :], lhsT=ones[:], rhs=gain_row[:], start=True, stop=True)
-        gains = const.tile([P, 2 * HEAD_DIM], F32)
-        plus = 2 * HEAD_DIM - HALF
-        nc.vector.tensor_scalar(
-            out=gains[:, 0:plus], in0=gain_ps[:, 0, 0:plus], scalar1=1.0, scalar2=None, op0=ALU.add
-        )
-        nc.vector.tensor_scalar(
-            out=gains[:, plus:],
-            in0=gain_ps[:, 0, plus:],
-            scalar1=-1.0,
-            scalar2=-1.0,
-            op0=ALU.mult,
-            op1=ALU.add,
-        )
-        table = const.tile([P, PARTS * SLOTS, 2, HEAD_DIM], F32)
-
-        def build_table(part, s0):
-            first = part * SLOTS + s0
-            for which in range(2):
-                nc.vector.tensor_tensor(
-                    out=table[:, first : first + GROUP, which, :].rearrange(
-                        "p s (h j) -> p s h j", h=2
-                    ),
-                    in0=cos_sin[:, which, part, s0 : s0 + GROUP, :]
-                    .unsqueeze(2)
-                    .to_broadcast([P, GROUP, 2, HALF]),
-                    in1=gains[:, which * HEAD_DIM : (which + 1) * HEAD_DIM]
-                    .rearrange("p (h j) -> p h j", h=2)
-                    .unsqueeze(1)
-                    .to_broadcast([P, GROUP, 2, HALF]),
-                    op=ALU.mult,
-                )
-
-        def quantise_group(i, s0):
-            grouped = stage.tile([P, GROUP * DIM], BF16, align_bytes=64)
-            grouped_words = grouped[:].bitcast(F32).rearrange("p (t r u) -> p t r u", t=GROUP, u=2)
-            for pair in range(0, GROUP, PAIR):
+        def quantise_quad(i, s0):
+            grouped = stage.tile([P, QUAD * DIM], BF16, align_bytes=64)
+            grouped_words = grouped[:].bitcast(F32).rearrange("p (t r u) -> p t r u", t=QUAD, u=2)
+            for pair in range(0, QUAD, PAIR):
                 xt = xt_pool.tile([P, PAIR, 2, P], F32)
                 for t in range(PAIR):
                     words = x_tiles[i][:, s0 + pair + t, :].bitcast(F32)
@@ -151,101 +119,133 @@ def tile_multiheadattention_pb_t_kernel(
                     out=grouped_words[:, pair : pair + PAIR],
                     in_=xt[:].rearrange("p t u r -> p t r u"),
                 )
-            x_codes = stage.tile([P, GROUP * P], U32, align_bytes=64)
-            x_scales = stage.tile([P, GROUP * P], U8, align_bytes=64)
-            nc.vector.quantize_mx(out=x_codes[:].bitcast(FP8X4), scales=x_scales[:], in_=grouped[:])
-            return x_codes, x_scales
-
-        def project_group(i, s0, x_codes, x_scales, k_out, v_out):
-            part = blocks[i][1]
-            sumsq = small.tile([P, GROUP * KV_HEADS], F32)
-            k_banks = []
-            for pair in range(0, GROUP, PAIR):
-                k_acc = k_pool.tile([P, PAIR, KV_COLS], F32)
-                v_acc = v_pool.tile([P, PAIR, KV_COLS], F32, tag="vacc")
-                k_banks.append(k_acc)
-                for w, acc in enumerate((k_acc, v_acc)):
-                    for t in range(PAIR):
-                        tokens = slice((pair + t) * P, (pair + t + 1) * P)
-                        nc.tensor.matmul_mx(
-                            out=acc[:, t, :],
-                            lhsT=x_codes[:, tokens].bitcast(FP8X4),
-                            lhsT_scale=x_scales[:, tokens],
-                            rhs=w_words[:, w, :].bitcast(FP4X4),
-                            rhs_scale=w_planes[:, w * KV_COLS : (w + 1) * KV_COLS],
-                            start=True,
-                            stop=True,
-                        )
-                for t in range(PAIR):
-                    for g in range(KV_HEADS):
-                        squares = small.tile([P, HEAD_DIM], F32)
-                        col = (pair + t) * KV_HEADS + g
-                        nc.scalar.activation(
-                            out=squares[:],
-                            in_=k_acc[:, t, g * HEAD_DIM : (g + 1) * HEAD_DIM],
-                            func=ACT.Square,
-                            accum_out=sumsq[:, col : col + 1],
-                        )
-                nc.scalar.copy(
-                    out=v_out[:, :, s0 + pair : s0 + pair + PAIR, :].rearrange("p g t d -> p t g d"),
-                    in_=v_acc[:].rearrange("p t (g d) -> p t g d", g=KV_HEADS),
-                )
-            rms = small.tile([P, GROUP * KV_HEADS], F32)
-            nc.scalar.activation(
-                out=rms[:], in_=sumsq[:], func=ACT.Sqrt, scale=1.0 / HEAD_DIM, bias=eps[:, 0:1]
+            columns = slice(s0 * P, (s0 + QUAD) * P)
+            nc.vector.quantize_mx(
+                out=x_codes[i][:, columns].bitcast(FP8X4),
+                scales=x_scales[i][:, columns],
+                in_=grouped[:],
             )
-            inv_rms = small.tile([P, GROUP * KV_HEADS], F32)
-            nc.vector.reciprocal(out=inv_rms[:], in_=rms[:])
-            products = stage.tile([P, KV_HEADS, GROUP, 2, HEAD_DIM], F32)
-            for t in range(GROUP):
-                for g in range(KV_HEADS):
-                    col = t * KV_HEADS + g
+
+        def project_quad(i, s0, w, g):
+            acc = acc_pool.tile([P, QUAD, HEAD_DIM], F32, name="acc")
+            for t in range(QUAD):
+                tokens = slice((s0 + t) * P, (s0 + t + 1) * P)
+                nc.tensor.matmul_mx(
+                    out=acc[:, t, :],
+                    lhsT=x_codes[i][:, tokens].bitcast(FP8X4),
+                    lhsT_scale=x_scales[i][:, tokens],
+                    rhs=w_words[:, w, 2 * g * HEAD_DIM : 2 * (g + 1) * HEAD_DIM].bitcast(FP4X4),
+                    rhs_scale=w_planes[
+                        :, w * KV_COLS + g * HEAD_DIM : w * KV_COLS + (g + 1) * HEAD_DIM
+                    ],
+                    start=True,
+                    stop=True,
+                )
+            return acc
+
+        def store_head(i, g, result, dram):
+            b, part = blocks[i]
+            for c in range(COPIES):
+                rows = dram[b, g * COPIES + c, part * BLOCK_TOKENS : (part + 1) * BLOCK_TOKENS, :]
+                nc.sync.dma_start(
+                    out=rows.rearrange("(p s) d -> p (s d)", s=SLOTS),
+                    in_=result[:].rearrange("p s d -> p (s d)"),
+                )
+
+        def value_head(i, g):
+            v_out = results.tile([P, SLOTS, HEAD_DIM], F32, name="v_out")
+            for s0 in range(0, SLOTS, QUAD):
+                acc = project_quad(i, s0, W_VALUE, g)
+                nc.scalar.copy(out=v_out[:, s0 : s0 + QUAD, :], in_=acc[:])
+            return v_out
+
+        gains = const.tile([P, 2, HEAD_DIM], F32)
+        table = const.tile([P, PARTS, SLOTS, 2, HEAD_DIM], F32)
+
+        def spread_gains():
+            gain_ps = acc_pool.tile([P, QUAD, HEAD_DIM], F32, name="acc")
+            spread = gain_ps[:].rearrange("p t d -> p (t d)")[:, 0 : 2 * HEAD_DIM]
+            nc.tensor.matmul(out=spread, lhsT=ones[:], rhs=gain_row[:], start=True, stop=True)
+            flat = gains[:].rearrange("p w d -> p (w d)")
+            plus = 2 * HEAD_DIM - HALF
+            nc.vector.tensor_scalar(
+                out=flat[:, 0:plus], in0=spread[:, 0:plus], scalar1=1.0, scalar2=None, op0=ALU.add
+            )
+            nc.vector.tensor_scalar(
+                out=flat[:, plus:],
+                in0=spread[:, plus:],
+                scalar1=-1.0,
+                scalar2=-1.0,
+                op0=ALU.mult,
+                op1=ALU.add,
+            )
+
+        def build_table(part):
+            for which in range(2):
+                nc.vector.tensor_tensor(
+                    out=table[:, part, :, which, :].rearrange("p s (h j) -> p s h j", h=2),
+                    in0=cos_sin[:, which, part, :, :]
+                    .unsqueeze(2)
+                    .to_broadcast([P, SLOTS, 2, HALF]),
+                    in1=gains[:, which, :]
+                    .rearrange("p (h j) -> p h j", h=2)
+                    .unsqueeze(1)
+                    .to_broadcast([P, SLOTS, 2, HALF]),
+                    op=ALU.mult,
+                )
+
+        def key_head(i, g):
+            part = blocks[i][1]
+            k_out = results.tile([P, SLOTS, HEAD_DIM], F32, name="k_out")
+            for s0 in range(0, SLOTS, QUAD):
+                acc = project_quad(i, s0, W_KEY, g)
+                sumsq = small.tile([P, QUAD], F32)
+                for t in range(QUAD):
+                    squares = small.tile([P, HEAD_DIM], F32)
+                    nc.scalar.activation(
+                        out=squares[:],
+                        in_=acc[:, t, :],
+                        func=ACT.Square,
+                        accum_out=sumsq[:, t : t + 1],
+                    )
+                rms = small.tile([P, QUAD], F32)
+                nc.scalar.activation(
+                    out=rms[:], in_=sumsq[:], func=ACT.Sqrt, scale=1.0 / HEAD_DIM, bias=eps[:, 0:1]
+                )
+                inv_rms = small.tile([P, QUAD], F32)
+                nc.vector.reciprocal(out=inv_rms[:], in_=rms[:])
+                products = stage.tile([P, QUAD, 2, HEAD_DIM], F32)
+                for t in range(QUAD):
                     nc.vector.scalar_tensor_tensor(
-                        out=products[:, g, t, :, :],
-                        in0=k_banks[t // PAIR][:, t % PAIR, g * HEAD_DIM : (g + 1) * HEAD_DIM]
-                        .unsqueeze(1)
-                        .to_broadcast([P, 2, HEAD_DIM]),
-                        scalar=inv_rms[:, col : col + 1],
-                        in1=table[:, part * SLOTS + s0 + t, :, :],
+                        out=products[:, t, :, :],
+                        in0=acc[:, t, :].unsqueeze(1).to_broadcast([P, 2, HEAD_DIM]),
+                        scalar=inv_rms[:, t : t + 1],
+                        in1=table[:, part, s0 + t, :, :],
                         op0=ALU.mult,
                         op1=ALU.mult,
                     )
-            for lo in (0, HALF):
-                other = HALF - lo
-                nc.gpsimd.tensor_tensor(
-                    out=k_out[:, :, s0 : s0 + GROUP, lo : lo + HALF],
-                    in0=products[:, :, :, 0, lo : lo + HALF],
-                    in1=products[:, :, :, 1, other : other + HALF],
-                    op=ALU.add,
-                )
+                for lo in (0, HALF):
+                    other = HALF - lo
+                    nc.gpsimd.tensor_tensor(
+                        out=k_out[:, s0 : s0 + QUAD, lo : lo + HALF],
+                        in0=products[:, :, 0, lo : lo + HALF],
+                        in1=products[:, :, 1, other : other + HALF],
+                        op=ALU.add,
+                    )
+            return k_out
 
-        def store(i, s0, slots, result, dram):
-            b, part = blocks[i]
-            heads = dram[b].rearrange("(g c) t d -> c g t d", c=COPIES)
-            for c in range(COPIES):
-                rows = heads[c][:, part * BLOCK_TOKENS : (part + 1) * BLOCK_TOKENS, :]
-                nc.sync.dma_start(
-                    out=rows.rearrange("g (p s) d -> p g s d", s=SLOTS)[:, :, s0 : s0 + slots, :],
-                    in_=result[:, :, s0 : s0 + slots, :],
-                )
-
-        outs = {}
-        ready = quantise_group(*groups[0])
-        for n, (i, s0) in enumerate(groups):
-            following = quantise_group(*groups[n + 1]) if n + 1 < len(groups) else None
-            b, part = blocks[i]
+        for s0 in range(0, SLOTS, QUAD):
+            quantise_quad(0, s0)
+        spread_gains()
+        keys_to_store = None
+        for i, (b, part) in enumerate(blocks):
             if b == 0:
-                build_table(part, s0)
-            if s0 == 0:
-                k_out = out_pool.tile([P, KV_HEADS, SLOTS, HEAD_DIM], F32, name="k_out")
-                v_out = out_pool.tile([P, KV_HEADS, SLOTS, HEAD_DIM], F32, name="v_out")
-                outs[i] = (k_out, v_out)
-            k_out, v_out = outs[i]
-            project_group(i, s0, ready[0], ready[1], k_out, v_out)
-            if i < BLOCKS_STORED_BY_GROUP:
-                store(i, s0, GROUP, v_out, out_1)
-                store(i, s0, GROUP, k_out, out_0)
-            elif s0 + GROUP == SLOTS:
-                store(i, 0, SLOTS, v_out, out_1)
-                store(i, 0, SLOTS, k_out, out_0)
-            ready = following
+                build_table(part)
+            for g in range(KV_HEADS):
+                if i + 1 < len(blocks):
+                    quantise_quad(i + 1, g * QUAD)
+                store_head(i, g, value_head(i, g), out_1)
+                if keys_to_store is not None:
+                    store_head(*keys_to_store)
+                keys_to_store = (i, g, key_head(i, g), out_0)
+        store_head(*keys_to_store)

@@ -145,12 +145,19 @@ def tile_multiheadattention_pb_t_kernel(
 
         def store_head(i, g, result, dram):
             b, part = blocks[i]
-            for c in range(COPIES):
-                rows = dram[b, g * COPIES + c, part * BLOCK_TOKENS : (part + 1) * BLOCK_TOKENS, :]
-                nc.sync.dma_start(
-                    out=rows.rearrange("(p s) d -> p (s d)", s=SLOTS),
-                    in_=result[:].rearrange("p s d -> p (s d)"),
-                )
+            rows = dram[
+                b,
+                g * COPIES : (g + 1) * COPIES,
+                part * BLOCK_TOKENS : (part + 1) * BLOCK_TOKENS,
+                :,
+            ]
+            nc.sync.dma_start(
+                out=rows.rearrange("c (p s) d -> p c (s d)", s=SLOTS),
+                in_=result[:]
+                .rearrange("p s d -> p (s d)")
+                .unsqueeze(1)
+                .to_broadcast([P, COPIES, SLOTS * HEAD_DIM]),
+            )
 
         def value_head(i, g):
             v_out = results.tile([P, SLOTS, HEAD_DIM], F32, name="v_out")

@@ -233,7 +233,7 @@ def tile_multiheadattention_pb_t_kernel(
                     )
                 for lo in (0, HALF):
                     other = HALF - lo
-                    nc.gpsimd.tensor_tensor(
+                    nc.vector.tensor_tensor(
                         out=k_out[:, s0 : s0 + QUAD, lo : lo + HALF],
                         in0=products[:, :, 0, lo : lo + HALF],
                         in1=products[:, :, 1, other : other + HALF],

@@ -54,7 +54,7 @@ def tile_multiheadattention_pb_t_kernel(
         eps = const.tile([P, 1], F32)
         nc.vector.memset(eps[:], EPS)
         warm = const.tile([P, 1], F32)
-        nc.scalar.activation(out=warm[:], in_=eps[:], func=ACT.Sqrt)
+        nc.scalar.activation(out=warm[:], in_=eps[:], func=ACT.Abs_reciprocal_sqrt)
         w_planes = const.tile([P, 2 * KV_COLS], U8, align_bytes=64)
         nc.vector.memset(w_planes[:].bitcast(I32), 0)
         gain_row = const.tile([P, 2 * HEAD_DIM], BF16)
@@ -204,6 +204,7 @@ def tile_multiheadattention_pb_t_kernel(
         def key_head(i, g):
             part = blocks[i][1]
             k_out = results.tile([P, SLOTS, HEAD_DIM], F32, name="k_out")
+            products = stage.tile([P, SLOTS, 2, HEAD_DIM], F32)
             for s0 in range(0, SLOTS, QUAD):
                 acc = project_quad(i, s0, W_KEY, g)
                 sumsq = small.tile([P, QUAD], F32)
@@ -215,30 +216,30 @@ def tile_multiheadattention_pb_t_kernel(
                         func=ACT.Square,
                         accum_out=sumsq[:, t : t + 1],
                     )
-                rms = small.tile([P, QUAD], F32)
-                nc.scalar.activation(
-                    out=rms[:], in_=sumsq[:], func=ACT.Sqrt, scale=1.0 / HEAD_DIM, bias=eps[:, 0:1]
-                )
                 inv_rms = small.tile([P, QUAD], F32)
-                nc.vector.reciprocal(out=inv_rms[:], in_=rms[:])
-                products = stage.tile([P, QUAD, 2, HEAD_DIM], F32)
+                nc.scalar.activation(
+                    out=inv_rms[:],
+                    in_=sumsq[:],
+                    func=ACT.Abs_reciprocal_sqrt,
+                    scale=1.0 / HEAD_DIM,
+                    bias=eps[:, 0:1],
+                )
                 for t in range(QUAD):
                     nc.vector.scalar_tensor_tensor(
-                        out=products[:, t, :, :],
+                        out=products[:, s0 + t, :, :],
                         in0=acc[:, t, :].unsqueeze(1).to_broadcast([P, 2, HEAD_DIM]),
                         scalar=inv_rms[:, t : t + 1],
                         in1=table[:, part, s0 + t, :, :],
                         op0=ALU.mult,
                         op1=ALU.mult,
                     )
-                for lo in (0, HALF):
-                    other = HALF - lo
-                    nc.vector.tensor_tensor(
-                        out=k_out[:, s0 : s0 + QUAD, lo : lo + HALF],
-                        in0=products[:, :, 0, lo : lo + HALF],
-                        in1=products[:, :, 1, other : other + HALF],
-                        op=ALU.add,
-                    )
+            halves = products[:].rearrange("p s w (h j) -> p s w h j", h=2)
+            nc.vector.tensor_tensor(
+                out=k_out[:].rearrange("p s (h j) -> p s h j", h=2),
+                in0=halves[:, :, 0, :, :],
+                in1=halves[:, :, 1, ::-1, :],
+                op=ALU.add,
+            )
             return k_out
 
         for s0 in range(0, SLOTS, QUAD):

@@ -143,7 +143,7 @@ def tile_multiheadattention_pb_t_kernel(
                 )
             return acc
 
-        def store_head(i, g, result, dram):
+        def store_head(i, g, result, dram, queue):
             b, part = blocks[i]
             rows = dram[
                 b,
@@ -151,7 +151,7 @@ def tile_multiheadattention_pb_t_kernel(
                 part * BLOCK_TOKENS : (part + 1) * BLOCK_TOKENS,
                 :,
             ]
-            nc.sync.dma_start(
+            queue.dma_start(
                 out=rows.rearrange("c (p s) d -> p c (s d)", s=SLOTS),
                 in_=result[:]
                 .rearrange("p s d -> p (s d)")
@@ -252,8 +252,8 @@ def tile_multiheadattention_pb_t_kernel(
             for g in range(KV_HEADS):
                 if i + 1 < len(blocks):
                     quantise_quad(i + 1, g * QUAD)
-                store_head(i, g, value_head(i, g), out_1)
+                store_head(i, g, value_head(i, g), out_1, nc.sync if i == 0 else nc.scalar)
                 if keys_to_store is not None:
                     store_head(*keys_to_store)
-                keys_to_store = (i, g, key_head(i, g), out_0)
+                keys_to_store = (i, g, key_head(i, g), out_0, nc.sync)
         store_head(*keys_to_store)

@@ -62,7 +62,7 @@ def tile_multiheadattention_pb_t_kernel(
 
         x_tiles, x_codes, x_scales = [], [], []
         for i in range(len(blocks)):
-            x_sb = per_block.tile([P, SLOTS, DIM], BF16, name="x_sb")
+            x_sb = per_block.tile([P, SLOTS, DIM], BF16, name="x_sb", align_bytes=256)
             codes = per_block.tile([P, SLOTS * P], U32, name="codes", align_bytes=64)
             scales = per_block.tile([P, SLOTS * P], U8, name="scales", align_bytes=64)
             x_tiles.append(x_sb)
@@ -86,8 +86,8 @@ def tile_multiheadattention_pb_t_kernel(
                     in_=scales[0, 4 * quadrant : 4 * quadrant + 4, :].bitcast(I32),
                 )
 
-        w_words = const.tile([P, 2, 2 * KV_COLS], U8, align_bytes=64)
-        cos_sin = const.tile([P, 2, PARTS, SLOTS, HALF], BF16)
+        w_words = const.tile([P, 2, 2 * KV_COLS], U8, align_bytes=256)
+        cos_sin = const.tile([P, 2, PARTS, SLOTS, HALF], BF16, align_bytes=256)
         load_x(0, 0, QUAD)
         for w, words in ((W_VALUE, Wv_words), (W_KEY, Wk_words)):
             nc.sync.dma_start(out=w_words[:, w, :].bitcast(I32), in_=words[0].bitcast(I32))
@@ -160,7 +160,7 @@ def tile_multiheadattention_pb_t_kernel(
             )
 
         def value_head(i, g):
-            v_out = results.tile([P, SLOTS, HEAD_DIM], F32, name="v_out")
+            v_out = results.tile([P, SLOTS, HEAD_DIM], F32, name="v_out", align_bytes=256)
             for s0 in range(0, SLOTS, QUAD):
                 acc = project_quad(i, s0, W_VALUE, g)
                 nc.scalar.copy(out=v_out[:, s0 : s0 + QUAD, :], in_=acc[:])
@@ -203,7 +203,7 @@ def tile_multiheadattention_pb_t_kernel(
 
         def key_head(i, g):
             part = blocks[i][1]
-            k_out = results.tile([P, SLOTS, HEAD_DIM], F32, name="k_out")
+            k_out = results.tile([P, SLOTS, HEAD_DIM], F32, name="k_out", align_bytes=256)
             products = stage.tile([P, SLOTS, 2, HEAD_DIM], F32)
             for s0 in range(0, SLOTS, QUAD):
                 acc = project_quad(i, s0, W_KEY, g)

@@ -143,7 +143,7 @@ def tile_multiheadattention_pb_t_kernel(
                 )
             return acc
 
-        def store_head(i, g, result, dram, queue):
+        def store_quad(i, g, s0, result, dram, queue):
             b, part = blocks[i]
             rows = dram[
                 b,
@@ -152,11 +152,13 @@ def tile_multiheadattention_pb_t_kernel(
                 :,
             ]
             queue.dma_start(
-                out=rows.rearrange("c (p s) d -> p c (s d)", s=SLOTS),
-                in_=result[:]
+                out=rows.rearrange("c (p s) d -> p c s d", s=SLOTS)[
+                    :, :, s0 : s0 + QUAD, :
+                ].rearrange("p c s d -> p c (s d)"),
+                in_=result[:, s0 : s0 + QUAD, :]
                 .rearrange("p s d -> p (s d)")
                 .unsqueeze(1)
-                .to_broadcast([P, COPIES, SLOTS * HEAD_DIM]),
+                .to_broadcast([P, COPIES, QUAD * HEAD_DIM]),
             )
 
         def value_head(i, g):
@@ -164,7 +166,7 @@ def tile_multiheadattention_pb_t_kernel(
             for s0 in range(0, SLOTS, QUAD):
                 acc = project_quad(i, s0, W_VALUE, g)
                 nc.scalar.copy(out=v_out[:, s0 : s0 + QUAD, :], in_=acc[:])
-            return v_out
+                store_quad(i, g, s0, v_out, out_1, nc.sync if i == 0 else nc.scalar)
 
         gains = const.tile([P, 2, HEAD_DIM], F32)
         table = const.tile([P, PARTS, SLOTS, 2, HEAD_DIM], F32)
@@ -233,14 +235,19 @@ def tile_multiheadattention_pb_t_kernel(
                         op0=ALU.mult,
                         op1=ALU.mult,
                     )
-            halves = products[:].rearrange("p s w (h j) -> p s w h j", h=2)
-            nc.vector.tensor_tensor(
-                out=k_out[:].rearrange("p s (h j) -> p s h j", h=2),
-                in0=halves[:, :, 0, :, :],
-                in1=halves[:, :, 1, ::-1, :],
-                op=ALU.add,
-            )
+                quad = slice(s0, s0 + QUAD)
+                halves = products[:, quad].rearrange("p s w (h j) -> p s w h j", h=2)
+                nc.vector.tensor_tensor(
+                    out=k_out[:, quad, :].rearrange("p s (h j) -> p s h j", h=2),
+                    in0=halves[:, :, 0, :, :],
+                    in1=halves[:, :, 1, ::-1, :],
+                    op=ALU.add,
+                )
             return k_out
+
+        def store_keys(i, g, k_out):
+            for s0 in range(0, SLOTS, QUAD):
+                store_quad(i, g, s0, k_out, out_0, nc.sync)
 
         for s0 in range(0, SLOTS, QUAD):
             quantise_quad(0, s0)
@@ -252,8 +259,8 @@ def tile_multiheadattention_pb_t_kernel(
             for g in range(KV_HEADS):
                 if i + 1 < len(blocks):
                     quantise_quad(i + 1, g * QUAD)
-                store_head(i, g, value_head(i, g), out_1, nc.sync if i == 0 else nc.scalar)
+                value_head(i, g)
                 if keys_to_store is not None:
-                    store_head(*keys_to_store)
-                keys_to_store = (i, g, key_head(i, g), out_0, nc.sync)
-        store_head(*keys_to_store)
+                    store_keys(*keys_to_store)
+                keys_to_store = (i, g, key_head(i, g))
+        store_keys(*keys_to_store)

@@ -189,25 +189,28 @@ def tile_multiheadattention_pb_t_kernel(
                 op1=ALU.add,
             )
 
-        def build_table(part):
+        def build_table(part, s0):
+            slots = slice(s0, s0 + QUAD)
             for which in range(2):
                 nc.vector.tensor_tensor(
-                    out=table[:, part, :, which, :].rearrange("p s (h j) -> p s h j", h=2),
-                    in0=cos_sin[:, which, part, :, :]
+                    out=table[:, part, slots, which, :].rearrange("p s (h j) -> p s h j", h=2),
+                    in0=cos_sin[:, which, part, slots, :]
                     .unsqueeze(2)
-                    .to_broadcast([P, SLOTS, 2, HALF]),
+                    .to_broadcast([P, QUAD, 2, HALF]),
                     in1=gains[:, which, :]
                     .rearrange("p (h j) -> p h j", h=2)
                     .unsqueeze(1)
-                    .to_broadcast([P, SLOTS, 2, HALF]),
+                    .to_broadcast([P, QUAD, 2, HALF]),
                     op=ALU.mult,
                 )
 
         def key_head(i, g):
-            part = blocks[i][1]
+            b, part = blocks[i]
             k_out = results.tile([P, SLOTS, HEAD_DIM], F32, name="k_out", align_bytes=256)
             products = stage.tile([P, SLOTS, 2, HEAD_DIM], F32)
             for s0 in range(0, SLOTS, QUAD):
+                if b == 0 and g == 0:
+                    build_table(part, s0)
                 acc = project_quad(i, s0, W_KEY, g)
                 sumsq = small.tile([P, QUAD], F32)
                 for t in range(QUAD):
@@ -235,6 +238,7 @@ def tile_multiheadattention_pb_t_kernel(
                         op0=ALU.mult,
                         op1=ALU.mult,
                     )
+            for s0 in range(0, SLOTS, QUAD):
                 quad = slice(s0, s0 + QUAD)
                 halves = products[:, quad].rearrange("p s w (h j) -> p s w h j", h=2)
                 nc.vector.tensor_tensor(
@@ -254,8 +258,6 @@ def tile_multiheadattention_pb_t_kernel(
         spread_gains()
         keys_to_store = None
         for i, (b, part) in enumerate(blocks):
-            if b == 0:
-                build_table(part)
             for g in range(KV_HEADS):
                 if i + 1 < len(blocks):
                     quantise_quad(i + 1, g * QUAD)

from contextlib import ExitStack

import concourse.mybir as mybir
from concourse.masks import make_identity

F32 = mybir.dt.float32
BF16 = mybir.dt.bfloat16
I32 = mybir.dt.int32
U32 = mybir.dt.uint32
U8 = mybir.dt.uint8
FP8X4 = mybir.dt.float8_e4m3fn_x4
FP4X4 = mybir.dt.float4_e2m1fn_x4
ACT = mybir.ActivationFunctionType
ALU = mybir.AluOpType

P = 128
BATCH, TOKENS, DIM = 2, 2048, 512
KV_HEADS, HEAD_DIM = 2, 128
COPIES = 2
HALF = HEAD_DIM // 2
KV_COLS = KV_HEADS * HEAD_DIM
EPS = 1e-6

WORDS = DIM // 2
SLOTS = 8
BLOCK_TOKENS = P * SLOTS
PARTS = TOKENS // BLOCK_TOKENS
PAIR = 2
QUAD = 4

FLOPS = 2 * BATCH * TOKENS * DIM * 2 * KV_COLS
W_KEY, W_VALUE = 0, 1


def tile_multiheadattention_pb_t_kernel(
    tc, kv_input, Wk_words, Wk_scales, Wv_words, Wv_scales, k_scale, cos, sin, out_0, out_1
):
    nc = tc.nc
    with ExitStack() as ctx:
        const = ctx.enter_context(tc.tile_pool(name="const", bufs=1))
        per_block = ctx.enter_context(tc.tile_pool(name="per_block", bufs=BATCH * PARTS))
        stage = ctx.enter_context(tc.tile_pool(name="stage", bufs=3))
        small = ctx.enter_context(tc.tile_pool(name="small", bufs=4))
        results = ctx.enter_context(tc.tile_pool(name="results", bufs=BATCH * PARTS * KV_HEADS))
        xt_pool = ctx.enter_context(tc.psum_pool(name="xt", bufs=2))
        acc_pool = ctx.enter_context(tc.psum_pool(name="acc", bufs=6))

        blocks = [(b, part) for part in range(PARTS) for b in range(BATCH)]

        identity = const.tile([P, P], F32)
        make_identity(nc, identity[:])
        ones = const.tile([P, P], BF16)
        nc.vector.memset(ones[:], 1.0)
        eps = const.tile([P, 1], F32)
        nc.vector.memset(eps[:], EPS)
        warm = const.tile([P, 1], F32)
        nc.scalar.activation(out=warm[:], in_=eps[:], func=ACT.Abs_reciprocal_sqrt)
        w_planes = const.tile([P, 2 * KV_COLS], U8, align_bytes=64)
        nc.vector.memset(w_planes[:].bitcast(I32), 0)
        gain_row = const.tile([P, 2 * HEAD_DIM], BF16)
        nc.vector.memset(gain_row[:], 0.0)

        x_tiles, x_codes, x_scales = [], [], []
        for i in range(len(blocks)):
            x_sb = per_block.tile([P, SLOTS, DIM], BF16, name="x_sb", align_bytes=256)
            codes = per_block.tile([P, SLOTS * P], U32, name="codes", align_bytes=64)
            scales = per_block.tile([P, SLOTS * P], U8, name="scales", align_bytes=64)
            x_tiles.append(x_sb)
            x_codes.append(codes)
            x_scales.append(scales)

        def load_x(i, s0, slots):
            b, part = blocks[i]
            rows = kv_input[b, part * BLOCK_TOKENS : (part + 1) * BLOCK_TOKENS, :]
            nc.sync.dma_start(
                out=x_tiles[i][:, s0 : s0 + slots, :],
                in_=rows.rearrange("(p s) k -> p s k", s=SLOTS)[:, s0 : s0 + slots, :],
            )

        def load_scales(w, scales):
            for quadrant in range(4):
                nc.sync.dma_start(
                    out=w_planes[
                        32 * quadrant : 32 * quadrant + 4, w * KV_COLS : (w + 1) * KV_COLS
                    ].bitcast(I32),
                    in_=scales[0, 4 * quadrant : 4 * quadrant + 4, :].bitcast(I32),
                )

        w_words = const.tile([P, 2, 2 * KV_COLS], U8, align_bytes=256)
        cos_sin = const.tile([P, 2, PARTS, SLOTS, HALF], BF16, align_bytes=256)
        load_x(0, 0, QUAD)
        for w, words in ((W_VALUE, Wv_words), (W_KEY, Wk_words)):
            nc.sync.dma_start(out=w_words[:, w, :].bitcast(I32), in_=words[0].bitcast(I32))
        load_scales(W_VALUE, Wv_scales)
        for s0 in range(QUAD, SLOTS, QUAD):
            load_x(0, s0, QUAD)
        for rep in range(2):
            nc.sync.dma_start(
                out=gain_row[0:1, rep * HEAD_DIM : (rep + 1) * HEAD_DIM], in_=k_scale.unsqueeze(0)
            )
        for which, angle in enumerate((cos, sin)):
            nc.sync.dma_start(
                out=cos_sin[:, which], in_=angle.rearrange("(h p s) j -> p h s j", h=PARTS, p=P)
            )
        load_scales(W_KEY, Wk_scales)
        for i in range(1, len(blocks)):
            load_x(i, 0, SLOTS)

        def quantise_quad(i, s0):
            grouped = stage.tile([P, QUAD * DIM], BF16, align_bytes=64)
            grouped_words = grouped[:].bitcast(F32).rearrange("p (t r u) -> p t r u", t=QUAD, u=2)
            for pair in range(0, QUAD, PAIR):
                xt = xt_pool.tile([P, PAIR, 2, P], F32)
                for t in range(PAIR):
                    words = x_tiles[i][:, s0 + pair + t, :].bitcast(F32)
                    for u in range(2):
                        nc.tensor.transpose(xt[:, t, u, :], words[:, u:WORDS:2], identity[:])
                nc.scalar.copy(
                    out=grouped_words[:, pair : pair + PAIR],
                    in_=xt[:].rearrange("p t u r -> p t r u"),
                )
            columns = slice(s0 * P, (s0 + QUAD) * P)
            nc.vector.quantize_mx(
                out=x_codes[i][:, columns].bitcast(FP8X4),
                scales=x_scales[i][:, columns],
                in_=grouped[:],
            )

        def project_quad(i, s0, w, g):
            acc = acc_pool.tile([P, QUAD, HEAD_DIM], F32, name="acc")
            for t in range(QUAD):
                tokens = slice((s0 + t) * P, (s0 + t + 1) * P)
                nc.tensor.matmul_mx(
                    out=acc[:, t, :],
                    lhsT=x_codes[i][:, tokens].bitcast(FP8X4),
                    lhsT_scale=x_scales[i][:, tokens],
                    rhs=w_words[:, w, 2 * g * HEAD_DIM : 2 * (g + 1) * HEAD_DIM].bitcast(FP4X4),
                    rhs_scale=w_planes[
                        :, w * KV_COLS + g * HEAD_DIM : w * KV_COLS + (g + 1) * HEAD_DIM
                    ],
                    start=True,
                    stop=True,
                )
            return acc

        def store_quad(i, g, s0, result, dram, queue):
            b, part = blocks[i]
            rows = dram[
                b,
                g * COPIES : (g + 1) * COPIES,
                part * BLOCK_TOKENS : (part + 1) * BLOCK_TOKENS,
                :,
            ]
            queue.dma_start(
                out=rows.rearrange("c (p s) d -> p c s d", s=SLOTS)[
                    :, :, s0 : s0 + QUAD, :
                ].rearrange("p c s d -> p c (s d)"),
                in_=result[:, s0 : s0 + QUAD, :]
                .rearrange("p s d -> p (s d)")
                .unsqueeze(1)
                .to_broadcast([P, COPIES, QUAD * HEAD_DIM]),
            )

        def value_head(i, g):
            v_out = results.tile([P, SLOTS, HEAD_DIM], F32, name="v_out", align_bytes=256)
            for s0 in range(0, SLOTS, QUAD):
                acc = project_quad(i, s0, W_VALUE, g)
                nc.scalar.copy(out=v_out[:, s0 : s0 + QUAD, :], in_=acc[:])
                store_quad(i, g, s0, v_out, out_1, nc.sync if i == 0 else nc.scalar)

        gains = const.tile([P, 2, HEAD_DIM], F32)
        table = const.tile([P, PARTS, SLOTS, 2, HEAD_DIM], F32)

        def spread_gains():
            gain_ps = acc_pool.tile([P, QUAD, HEAD_DIM], F32, name="acc")
            spread = gain_ps[:].rearrange("p t d -> p (t d)")[:, 0 : 2 * HEAD_DIM]
            nc.tensor.matmul(out=spread, lhsT=ones[:], rhs=gain_row[:], start=True, stop=True)
            flat = gains[:].rearrange("p w d -> p (w d)")
            plus = 2 * HEAD_DIM - HALF
            nc.vector.tensor_scalar(
                out=flat[:, 0:plus], in0=spread[:, 0:plus], scalar1=1.0, scalar2=None, op0=ALU.add
            )
            nc.vector.tensor_scalar(
                out=flat[:, plus:],
                in0=spread[:, plus:],
                scalar1=-1.0,
                scalar2=-1.0,
                op0=ALU.mult,
                op1=ALU.add,
            )

        def build_table(part, s0):
            slots = slice(s0, s0 + QUAD)
            for which in range(2):
                nc.vector.tensor_tensor(
                    out=table[:, part, slots, which, :].rearrange("p s (h j) -> p s h j", h=2),
                    in0=cos_sin[:, which, part, slots, :]
                    .unsqueeze(2)
                    .to_broadcast([P, QUAD, 2, HALF]),
                    in1=gains[:, which, :]
                    .rearrange("p (h j) -> p h j", h=2)
                    .unsqueeze(1)
                    .to_broadcast([P, QUAD, 2, HALF]),
                    op=ALU.mult,
                )

        def key_head(i, g):
            b, part = blocks[i]
            k_out = results.tile([P, SLOTS, HEAD_DIM], F32, name="k_out", align_bytes=256)
            products = stage.tile([P, SLOTS, 2, HEAD_DIM], F32)
            for s0 in range(0, SLOTS, QUAD):
                if b == 0 and g == 0:
                    build_table(part, s0)
                acc = project_quad(i, s0, W_KEY, g)
                sumsq = small.tile([P, QUAD], F32)
                for t in range(QUAD):
                    squares = small.tile([P, HEAD_DIM], F32)
                    nc.scalar.activation(
                        out=squares[:],
                        in_=acc[:, t, :],
                        func=ACT.Square,
                        accum_out=sumsq[:, t : t + 1],
                    )
                inv_rms = small.tile([P, QUAD], F32)
                nc.scalar.activation(
                    out=inv_rms[:],
                    in_=sumsq[:],
                    func=ACT.Abs_reciprocal_sqrt,
                    scale=1.0 / HEAD_DIM,
                    bias=eps[:, 0:1],
                )
                for t in range(QUAD):
                    nc.vector.scalar_tensor_tensor(
                        out=products[:, s0 + t, :, :],
                        in0=acc[:, t, :].unsqueeze(1).to_broadcast([P, 2, HEAD_DIM]),
                        scalar=inv_rms[:, t : t + 1],
                        in1=table[:, part, s0 + t, :, :],
                        op0=ALU.mult,
                        op1=ALU.mult,
                    )
            for s0 in range(0, SLOTS, QUAD):
                quad = slice(s0, s0 + QUAD)
                halves = products[:, quad].rearrange("p s w (h j) -> p s w h j", h=2)
                nc.vector.tensor_tensor(
                    out=k_out[:, quad, :].rearrange("p s (h j) -> p s h j", h=2),
                    in0=halves[:, :, 0, :, :],
                    in1=halves[:, :, 1, ::-1, :],
                    op=ALU.add,
                )
            return k_out

        def store_keys(i, g, k_out):
            for s0 in range(0, SLOTS, QUAD):
                store_quad(i, g, s0, k_out, out_0, nc.sync)

        for s0 in range(0, SLOTS, QUAD):
            quantise_quad(0, s0)
        spread_gains()
        keys_to_store = None
        for i, (b, part) in enumerate(blocks):
            for g in range(KV_HEADS):
                if i + 1 < len(blocks):
                    quantise_quad(i + 1, g * QUAD)
                value_head(i, g)
                if keys_to_store is not None:
                    store_keys(*keys_to_store)
                keys_to_store = (i, g, key_head(i, g))
        store_keys(*keys_to_store)
